import numpy as np
import ml_dtypes


def mxq(x, axis, fmt="e4m3"):
    dtype, down = {"e4m3": (ml_dtypes.float8_e4m3fn, 7), "e5m2": (ml_dtypes.float8_e5m2, 14)}[fmt]
    v = np.moveaxis(np.asarray(x, np.float32).astype(ml_dtypes.bfloat16).astype(np.float64), axis, -1)
    blocks = v.reshape(v.shape[:-1] + (-1, 32))
    amax = np.abs(blocks).max(-1, keepdims=True)
    byte = np.maximum(np.where(amax > 0, np.frexp(amax)[1] - 1 + 127, 0) - down, 1)
    scale = np.exp2(byte - 127.0)
    codes = (blocks / scale).astype(np.float32).astype(dtype).astype(np.float64)
    return np.moveaxis((codes * scale).reshape(v.shape), -1, axis)


WIDE = False


def mx_kscale(k):
    if not WIDE:
        return np.ones(k)
    levels = np.array([10, -10, 5, -5, 0])
    a = np.random.permutation(np.resize(levels, k // 512 * 4)).reshape(k // 512, 4)
    idx = np.arange(k)
    return np.exp2(a[idx // 512, idx % 128 // 32])


BF16 = ml_dtypes.bfloat16


def bf(x):
    return np.asarray(x, np.float32).astype(BF16)


def f64(x):
    return np.asarray(x).astype(np.float64)


B, C, D, O = 2, 256, 4096, 512
S0 = 1
S = 2
P = D // (S * (S0 + 1))
K = S * C


def setup_inputs():
    s = mx_kscale(K).reshape(S, C)
    sx = np.tile(np.repeat(s.T, S0 + 1, axis=1), (1, P))
    return {"x": bf(np.random.standard_normal((B, C, D)) * sx),
            "weight": bf(np.random.standard_normal((O, C, 1, S)) / C ** 0.25 / s.T[None, :, None, :])}


def reference(x, weight):
    xp = f64(x).reshape(B, C, D // (S0 + 1), S0 + 1).sum(axis=-1)
    xr = xp.reshape(B, C, P, S)
    a = xr.transpose(0, 2, 3, 1).reshape(B, P, K)
    w = f64(weight)[:, :, 0, :].transpose(2, 1, 0).reshape(K, O)
    out = (mxq(a, 2, "e4m3") @ mxq(w, 0, "e4m3")) / np.sqrt(C)
    return out.transpose(0, 2, 1)

@@ -1,0 +1,142 @@
+from contextlib import ExitStack
+
+import concourse.mybir as mybir
+from concourse.masks import make_identity
+
+BF16 = mybir.dt.bfloat16
+F32 = mybir.dt.float32
+U32 = mybir.dt.uint32
+U8 = mybir.dt.uint8
+FP8X4 = mybir.dt.float8_e4m3fn_x4
+ADD = mybir.AluOpType.add
+COPY = mybir.ActivationFunctionType.Copy
+
+P = 128
+BATCH, CH, POS, OUTC = 2, 256, 4096, 512
+NPOS = POS // 4
+OT = OUTC // P
+FLOPS = 2 * BATCH * NPOS * (2 * CH) * OUTC
+INV = 1.0 / 16.0
+
+LOADS = [(0, 0, 128), (0, 128, 128), (0, 256, 256), (0, 512, 512), (1, 0, 512), (1, 512, 512)]
+UNITS = [
+    (0, 0, 128),
+    (0, 128, 128),
+    (0, 256, 256),
+    (0, 512, 256),
+    (0, 768, 256),
+    (1, 0, 256),
+    (1, 256, 256),
+    (1, 512, 256),
+    (1, 768, 256),
+]
+STORES = {2: (0, 0, 512), 4: (0, 512, 1024), 6: (1, 0, 512), 8: (1, 512, 1024)}
+
+
+def tile_nonoverlappingconv1d_shared_kernel(tc, x, weight, out):
+    nc = tc.nc
+    with ExitStack() as ctx:
+        ctx.enter_context(tc.manual_schedule())
+        keep = ctx.enter_context(tc.tile_pool(name="keep", bufs=1))
+        psum_w = ctx.enter_context(tc.psum_pool(name="psum_w", bufs=2))
+        psum = ctx.enter_context(tc.psum_pool(name="psum", bufs=6))
+
+        w_sb = keep.tile([P, OT * 2 * CH], BF16, name="w_sb")
+        nc.sync.dma_start(out=w_sb[:], in_=weight.rearrange("(p a) c one k -> p (a c one k)", a=OT))
+        x_tiles = []
+        for i, (b, n0, w) in enumerate(LOADS):
+            xt = keep.tile([P, 2, 4 * w], BF16, name="x%d" % i)
+            nc.sync.dma_start(
+                out=xt[:],
+                in_=x[b].rearrange("(h p) d -> p h d", p=P)[:, :, 4 * n0 : 4 * (n0 + w)],
+            )
+            x_tiles.append(xt)
+
+        ident = keep.tile([P, P], F32, name="ident")
+        make_identity(nc, ident[:])
+        warm_in = keep.tile([P, 1], F32, name="warm_in")
+        warm_out = keep.tile([P, 1], F32, name="warm_out")
+        nc.vector.memset(warm_in[:], 0.0)
+        nc.scalar.activation(out=warm_out[:], in_=warm_in[:], func=COPY, scale=1.0)
+
+        w_words = w_sb[:].bitcast(F32)
+        w_grouped = keep.tile([P, OT * P * 4], BF16, name="w_grouped", align_bytes=64)
+        wg_words = w_grouped[:].bitcast(F32)
+        w_codes = keep.tile([P, OT * P], U32, name="w_codes", align_bytes=64)
+        w_scales = keep.tile([P, OT * P], U8, name="w_scales", align_bytes=64)
+        for g in range(2):
+            wT = psum_w.tile([P, 512], F32, name="wT")
+            for q in range(4):
+                col = g * 512 + q * P
+                nc.tensor.transpose(wT[:, q * P : (q + 1) * P], w_words[:, col : col + P], ident[:])
+            nc.scalar.copy(
+                out=wg_words[:, g * 512 : (g + 1) * 512].rearrange("p (a o h) -> p a o h", a=2, h=2),
+                in_=wT[:].rearrange("p (a h o) -> p a o h", a=2, h=2),
+            )
+
+        out_sb = [keep.tile([P, OT, NPOS], F32, name="out_sb%d" % b) for b in range(BATCH)]
+        out_view = [out[b].rearrange("(p a) n -> p a n", a=OT) for b in range(BATCH)]
+        grouped = {}
+        codes = {}
+        scales = {}
+
+        def add(u):
+            b, n0, w = UNITS[u]
+            i = [j for j, (lb, l0, lw) in enumerate(LOADS) if lb == b and l0 <= n0 < l0 + lw][0]
+            off = 4 * (n0 - LOADS[i][1])
+            src = x_tiles[i][:, :, off : off + 4 * w].rearrange("p h (n k e) -> p n h k e", k=2, e=2)
+            g = keep.tile([P, 4 * w], BF16, name="g%d" % u, align_bytes=64)
+            nc.vector.tensor_tensor(
+                out=g[:].rearrange("p (n h k) -> p n h k", h=2, k=2),
+                in0=src[:, :, :, :, 0],
+                in1=src[:, :, :, :, 1],
+                op=ADD,
+            )
+            grouped[u] = g
+
+        def quant(u):
+            w = UNITS[u][2]
+            c = keep.tile([P, w], U32, name="c%d" % u, align_bytes=64)
+            s = keep.tile([P, w], U8, name="s%d" % u, align_bytes=64)
+            nc.vector.quantize_mx(out=c[:].bitcast(FP8X4), scales=s[:], in_=grouped[u][:])
+            codes[u] = c
+            scales[u] = s
+
+        def multiply(u, last):
+            b, n0, w = UNITS[u]
+            ga = 512 // w
+            for j0 in range(0, OT, ga):
+                acc = psum.tile([P, 512], F32, name="acc")
+                for j in range(ga):
+                    a = j0 + j
+                    nc.tensor.matmul_mx(
+                        out=acc[:, j * w : (j + 1) * w],
+                        lhsT=w_codes[:, a * P : (a + 1) * P].bitcast(FP8X4),
+                        lhsT_scale=w_scales[:, a * P : (a + 1) * P],
+                        rhs=codes[u][:].bitcast(FP8X4),
+                        rhs_scale=scales[u][:],
+                        start=True,
+                        stop=True,
+                    )
+                dst = out_sb[b][:, j0 : j0 + ga, n0 : n0 + w]
+                srcv = acc[:].rearrange("p (a n) -> p a n", a=ga)
+                if last and j0 > 0:
+                    nc.vector.tensor_scalar_mul(out=dst, in0=srcv, scalar1=INV)
+                else:
+                    nc.scalar.activation(out=dst, in_=srcv, func=COPY, scale=INV)
+            if u in STORES:
+                sb, s0, s1 = STORES[u]
+                nc.sync.dma_start(out=out_view[sb][:, :, s0:s1], in_=out_sb[sb][:, :, s0:s1])
+
+        n_units = len(UNITS)
+        add(0)
+        add(1)
+        nc.vector.quantize_mx(out=w_codes[:].bitcast(FP8X4), scales=w_scales[:], in_=w_grouped[:])
+        quant(0)
+        multiply(0, False)
+        for u in range(2, n_units):
+            add(u)
+            quant(u - 1)
+            multiply(u - 1, False)
+        quant(n_units - 1)
+        multiply(n_units - 1, True)

@@ -30,7 +30,17 @@ UNITS = [
     (1, 512, 256),
     (1, 768, 256),
 ]
-STORES = {2: (0, 0, 512), 4: (0, 512, 1024), 6: (1, 0, 512), 8: (1, 512, 1024)}
+STORES = {
+    (2, 0): (0, 0, 2, 0, 512),
+    (2, 2): (0, 2, 2, 0, 512),
+    (4, 0): (0, 0, 2, 512, 1024),
+    (4, 2): (0, 2, 2, 512, 1024),
+    (6, 0): (1, 0, 2, 0, 512),
+    (6, 2): (1, 2, 2, 0, 512),
+    (7, 2): (1, 0, 4, 512, 768),
+    (8, 2): (1, 0, 4, 768, 1024),
+}
+ON_VECTOR = [(7, 2), (8, 2)]
 
 
 def tile_nonoverlappingconv1d_shared_kernel(tc, x, weight, out):
@@ -102,7 +112,7 @@ def tile_nonoverlappingconv1d_shared_kernel(tc, x, weight, out):
             codes[u] = c
             scales[u] = s
 
-        def multiply(u, last):
+        def multiply(u):
             b, n0, w = UNITS[u]
             ga = 512 // w
             for j0 in range(0, OT, ga):
@@ -120,23 +130,37 @@ def tile_nonoverlappingconv1d_shared_kernel(tc, x, weight, out):
                     )
                 dst = out_sb[b][:, j0 : j0 + ga, n0 : n0 + w]
                 srcv = acc[:].rearrange("p (a n) -> p a n", a=ga)
-                if last and j0 > 0:
+                if (u, j0) in ON_VECTOR:
                     nc.vector.tensor_scalar_mul(out=dst, in0=srcv, scalar1=INV)
                 else:
                     nc.scalar.activation(out=dst, in_=srcv, func=COPY, scale=INV)
-            if u in STORES:
-                sb, s0, s1 = STORES[u]
-                nc.sync.dma_start(out=out_view[sb][:, :, s0:s1], in_=out_sb[sb][:, :, s0:s1])
+                if (u, j0) in STORES:
+                    sb, a0, na, s0, s1 = STORES[(u, j0)]
+                    nc.sync.dma_start(
+                        out=out_view[sb][:, a0 : a0 + na, s0:s1], in_=out_sb[sb][:, a0 : a0 + na, s0:s1]
+                    )
 
-        n_units = len(UNITS)
+        def quant_w(g):
+            nc.vector.quantize_mx(
+                out=w_codes[:, g * 256 : (g + 1) * 256].bitcast(FP8X4),
+                scales=w_scales[:, g * 256 : (g + 1) * 256],
+                in_=w_grouped[:, g * 1024 : (g + 1) * 1024],
+            )
+
         add(0)
         add(1)
-        nc.vector.quantize_mx(out=w_codes[:].bitcast(FP8X4), scales=w_scales[:], in_=w_grouped[:])
-        quant(0)
-        multiply(0, False)
-        for u in range(2, n_units):
+        quant_w(0)
+        quant_w(1)
+        add(2)
+        for u in range(3):
+            quant(u)
+            multiply(u)
+        add(3)
+        for u in range(4, len(UNITS)):
             add(u)
             quant(u - 1)
-            multiply(u - 1, False)
-        quant(n_units - 1)
-        multiply(n_units - 1, True)
+            if u - 1 < 7:
+                multiply(u - 1)
+        quant(8)
+        multiply(7)
+        multiply(8)

@@ -18,7 +18,8 @@ OT = OUTC // P
 FLOPS = 2 * BATCH * NPOS * (2 * CH) * OUTC
 INV = 1.0 / 16.0
 
-LOADS = [(0, 0, 128), (0, 128, 128), (0, 256, 256), (0, 512, 512), (1, 0, 512), (1, 512, 512)]
+LOADS = [(0, 0, 128), (0, 128, 128), (0, 256, 256), (0, 512, 256), (0, 768, 256), (1, 0, 512), (1, 512, 512)]
+HELP = {1: 128, 2: 128, 3: 128}
 UNITS = [
     (0, 0, 128),
     (0, 128, 128),
@@ -64,6 +65,8 @@ def tile_nonoverlappingconv1d_shared_kernel(tc, x, weight, out):
 
         ident = keep.tile([P, P], F32, name="ident")
         make_identity(nc, ident[:])
+        ident_b = keep.tile([P, P], BF16, name="ident_b")
+        make_identity(nc, ident_b[:])
         warm_in = keep.tile([P, 1], F32, name="warm_in")
         warm_out = keep.tile([P, 1], F32, name="warm_out")
         nc.vector.memset(warm_in[:], 0.0)
@@ -90,19 +93,44 @@ def tile_nonoverlappingconv1d_shared_kernel(tc, x, weight, out):
         codes = {}
         scales = {}
 
-        def add(u):
-            b, n0, w = UNITS[u]
+        def x_part(b, n0, w):
             i = [j for j, (lb, l0, lw) in enumerate(LOADS) if lb == b and l0 <= n0 < l0 + lw][0]
             off = 4 * (n0 - LOADS[i][1])
-            src = x_tiles[i][:, :, off : off + 4 * w].rearrange("p h (n k e) -> p n h k e", k=2, e=2)
-            g = keep.tile([P, 4 * w], BF16, name="g%d" % u, align_bytes=64)
+            return x_tiles[i][:, :, off : off + 4 * w]
+
+        for u, (b, n0, w) in enumerate(UNITS):
+            grouped[u] = keep.tile([P, 4 * w], BF16, name="g%d" % u, align_bytes=64)
+
+        def add(u):
+            b, n0, w = UNITS[u]
+            vw = w - HELP.get(u, 0)
+            src = x_part(b, n0, vw).rearrange("p h (n k e) -> p n h k e", k=2, e=2)
             nc.vector.tensor_tensor(
-                out=g[:].rearrange("p (n h k) -> p n h k", h=2, k=2),
+                out=grouped[u][:, : 4 * vw].rearrange("p (n h k) -> p n h k", h=2, k=2),
                 in0=src[:, :, :, :, 0],
                 in1=src[:, :, :, :, 1],
                 op=ADD,
             )
-            grouped[u] = g
+
+        def help_add(u):
+            b, n0, w = UNITS[u]
+            hw = HELP[u]
+            vw = w - hw
+            src = x_part(b, n0 + vw, hw).rearrange("p h (m e) -> p h m e", e=2)
+            hb = psum_w.tile([P, 512], F32, name="wT")
+            for h in range(2):
+                for e in range(2):
+                    nc.tensor.matmul(
+                        out=hb[:, h * 2 * hw : (h + 1) * 2 * hw],
+                        lhsT=ident_b[:],
+                        rhs=src[:, h, :, e],
+                        start=(e == 0),
+                        stop=(e == 1),
+                    )
+            nc.scalar.copy(
+                out=grouped[u][:, 4 * vw : 4 * w].rearrange("p (n h k) -> p n h k", h=2, k=2),
+                in_=hb[:].rearrange("p (h n k) -> p n h k", h=2, k=2),
+            )
 
         def quant(u):
             w = UNITS[u][2]
@@ -148,14 +176,19 @@ def tile_nonoverlappingconv1d_shared_kernel(tc, x, weight, out):
             )
 
         add(0)
-        add(1)
+        help_add(1)
         quant_w(0)
         quant_w(1)
         add(2)
-        for u in range(3):
-            quant(u)
-            multiply(u)
+        help_add(2)
+        help_add(3)
+        quant(0)
+        multiply(0)
+        quant(1)
+        multiply(1)
         add(3)
+        quant(2)
+        multiply(2)
         for u in range(4, len(UNITS)):
             add(u)
             quant(u - 1)

@@ -18,7 +18,7 @@ OT = OUTC // P
 FLOPS = 2 * BATCH * NPOS * (2 * CH) * OUTC
 INV = 1.0 / 16.0
 
-LOADS = [(0, 0, 128), (0, 128, 128), (0, 256, 256), (0, 512, 256), (0, 768, 256), (1, 0, 512), (1, 512, 512)]
+LOADS = [(0, 0, 128), (0, 128, 384), (0, 512, 512), (1, 0, 512), (1, 512, 512)]
 HELP = {1: 128, 2: 128, 3: 128}
 UNITS = [
     (0, 0, 128),
@@ -38,8 +38,8 @@ STORES = {
     (4, 2): (0, 2, 2, 512, 1024),
     (6, 0): (1, 0, 2, 0, 512),
     (6, 2): (1, 2, 2, 0, 512),
-    (7, 2): (1, 0, 4, 512, 768),
-    (8, 2): (1, 0, 4, 768, 1024),
+    (8, 0): (1, 0, 2, 512, 1024),
+    (8, 2): (1, 2, 2, 512, 1024),
 }
 ON_VECTOR = [(7, 2), (8, 2)]
 

from contextlib import ExitStack

import concourse.mybir as mybir
from concourse.masks import make_identity

BF16 = mybir.dt.bfloat16
F32 = mybir.dt.float32
U32 = mybir.dt.uint32
U8 = mybir.dt.uint8
FP8X4 = mybir.dt.float8_e4m3fn_x4
ADD = mybir.AluOpType.add
COPY = mybir.ActivationFunctionType.Copy

P = 128
BATCH, CH, POS, OUTC = 2, 256, 4096, 512
NPOS = POS // 4
OT = OUTC // P
FLOPS = 2 * BATCH * NPOS * (2 * CH) * OUTC
INV = 1.0 / 16.0

LOADS = [(0, 0, 128), (0, 128, 384), (0, 512, 512), (1, 0, 512), (1, 512, 512)]
HELP = {1: 128, 2: 128, 3: 128}
UNITS = [
    (0, 0, 128),
    (0, 128, 128),
    (0, 256, 256),
    (0, 512, 256),
    (0, 768, 256),
    (1, 0, 256),
    (1, 256, 256),
    (1, 512, 256),
    (1, 768, 256),
]
STORES = {
    (2, 0): (0, 0, 2, 0, 512),
    (2, 2): (0, 2, 2, 0, 512),
    (4, 0): (0, 0, 2, 512, 1024),
    (4, 2): (0, 2, 2, 512, 1024),
    (6, 0): (1, 0, 2, 0, 512),
    (6, 2): (1, 2, 2, 0, 512),
    (8, 0): (1, 0, 2, 512, 1024),
    (8, 2): (1, 2, 2, 512, 1024),
}
ON_VECTOR = [(7, 2), (8, 2)]


def tile_nonoverlappingconv1d_shared_kernel(tc, x, weight, out):
    nc = tc.nc
    with ExitStack() as ctx:
        ctx.enter_context(tc.manual_schedule())
        keep = ctx.enter_context(tc.tile_pool(name="keep", bufs=1))
        psum_w = ctx.enter_context(tc.psum_pool(name="psum_w", bufs=2))
        psum = ctx.enter_context(tc.psum_pool(name="psum", bufs=6))

        w_sb = keep.tile([P, OT * 2 * CH], BF16, name="w_sb")
        nc.sync.dma_start(out=w_sb[:], in_=weight.rearrange("(p a) c one k -> p (a c one k)", a=OT))
        x_tiles = []
        for i, (b, n0, w) in enumerate(LOADS):
            xt = keep.tile([P, 2, 4 * w], BF16, name="x%d" % i)
            nc.sync.dma_start(
                out=xt[:],
                in_=x[b].rearrange("(h p) d -> p h d", p=P)[:, :, 4 * n0 : 4 * (n0 + w)],
            )
            x_tiles.append(xt)

        ident = keep.tile([P, P], F32, name="ident")
        make_identity(nc, ident[:])
        ident_b = keep.tile([P, P], BF16, name="ident_b")
        make_identity(nc, ident_b[:])
        warm_in = keep.tile([P, 1], F32, name="warm_in")
        warm_out = keep.tile([P, 1], F32, name="warm_out")
        nc.vector.memset(warm_in[:], 0.0)
        nc.scalar.activation(out=warm_out[:], in_=warm_in[:], func=COPY, scale=1.0)

        w_words = w_sb[:].bitcast(F32)
        w_grouped = keep.tile([P, OT * P * 4], BF16, name="w_grouped", align_bytes=64)
        wg_words = w_grouped[:].bitcast(F32)
        w_codes = keep.tile([P, OT * P], U32, name="w_codes", align_bytes=64)
        w_scales = keep.tile([P, OT * P], U8, name="w_scales", align_bytes=64)
        for g in range(2):
            wT = psum_w.tile([P, 512], F32, name="wT")
            for q in range(4):
                col = g * 512 + q * P
                nc.tensor.transpose(wT[:, q * P : (q + 1) * P], w_words[:, col : col + P], ident[:])
            nc.scalar.copy(
                out=wg_words[:, g * 512 : (g + 1) * 512].rearrange("p (a o h) -> p a o h", a=2, h=2),
                in_=wT[:].rearrange("p (a h o) -> p a o h", a=2, h=2),
            )

        out_sb = [keep.tile([P, OT, NPOS], F32, name="out_sb%d" % b) for b in range(BATCH)]
        out_view = [out[b].rearrange("(p a) n -> p a n", a=OT) for b in range(BATCH)]
        grouped = {}
        codes = {}
        scales = {}

        def x_part(b, n0, w):
            i = [j for j, (lb, l0, lw) in enumerate(LOADS) if lb == b and l0 <= n0 < l0 + lw][0]
            off = 4 * (n0 - LOADS[i][1])
            return x_tiles[i][:, :, off : off + 4 * w]

        for u, (b, n0, w) in enumerate(UNITS):
            grouped[u] = keep.tile([P, 4 * w], BF16, name="g%d" % u, align_bytes=64)

        def add(u):
            b, n0, w = UNITS[u]
            vw = w - HELP.get(u, 0)
            src = x_part(b, n0, vw).rearrange("p h (n k e) -> p n h k e", k=2, e=2)
            nc.vector.tensor_tensor(
                out=grouped[u][:, : 4 * vw].rearrange("p (n h k) -> p n h k", h=2, k=2),
                in0=src[:, :, :, :, 0],
                in1=src[:, :, :, :, 1],
                op=ADD,
            )

        def help_add(u):
            b, n0, w = UNITS[u]
            hw = HELP[u]
            vw = w - hw
            src = x_part(b, n0 + vw, hw).rearrange("p h (m e) -> p h m e", e=2)
            hb = psum_w.tile([P, 512], F32, name="wT")
            for h in range(2):
                for e in range(2):
                    nc.tensor.matmul(
                        out=hb[:, h * 2 * hw : (h + 1) * 2 * hw],
                        lhsT=ident_b[:],
                        rhs=src[:, h, :, e],
                        start=(e == 0),
                        stop=(e == 1),
                    )
            nc.scalar.copy(
                out=grouped[u][:, 4 * vw : 4 * w].rearrange("p (n h k) -> p n h k", h=2, k=2),
                in_=hb[:].rearrange("p (h n k) -> p n h k", h=2, k=2),
            )

        def quant(u):
            w = UNITS[u][2]
            c = keep.tile([P, w], U32, name="c%d" % u, align_bytes=64)
            s = keep.tile([P, w], U8, name="s%d" % u, align_bytes=64)
            nc.vector.quantize_mx(out=c[:].bitcast(FP8X4), scales=s[:], in_=grouped[u][:])
            codes[u] = c
            scales[u] = s

        def multiply(u):
            b, n0, w = UNITS[u]
            ga = 512 // w
            for j0 in range(0, OT, ga):
                acc = psum.tile([P, 512], F32, name="acc")
                for j in range(ga):
                    a = j0 + j
                    nc.tensor.matmul_mx(
                        out=acc[:, j * w : (j + 1) * w],
                        lhsT=w_codes[:, a * P : (a + 1) * P].bitcast(FP8X4),
                        lhsT_scale=w_scales[:, a * P : (a + 1) * P],
                        rhs=codes[u][:].bitcast(FP8X4),
                        rhs_scale=scales[u][:],
                        start=True,
                        stop=True,
                    )
                dst = out_sb[b][:, j0 : j0 + ga, n0 : n0 + w]
                srcv = acc[:].rearrange("p (a n) -> p a n", a=ga)
                if (u, j0) in ON_VECTOR:
                    nc.vector.tensor_scalar_mul(out=dst, in0=srcv, scalar1=INV)
                else:
                    nc.scalar.activation(out=dst, in_=srcv, func=COPY, scale=INV)
                if (u, j0) in STORES:
                    sb, a0, na, s0, s1 = STORES[(u, j0)]
                    nc.sync.dma_start(
                        out=out_view[sb][:, a0 : a0 + na, s0:s1], in_=out_sb[sb][:, a0 : a0 + na, s0:s1]
                    )

        def quant_w(g):
            nc.vector.quantize_mx(
                out=w_codes[:, g * 256 : (g + 1) * 256].bitcast(FP8X4),
                scales=w_scales[:, g * 256 : (g + 1) * 256],
                in_=w_grouped[:, g * 1024 : (g + 1) * 1024],
            )

        add(0)
        help_add(1)
        quant_w(0)
        quant_w(1)
        add(2)
        help_add(2)
        help_add(3)
        quant(0)
        multiply(0)
        quant(1)
        multiply(1)
        add(3)
        quant(2)
        multiply(2)
        for u in range(4, len(UNITS)):
            add(u)
            quant(u - 1)
            if u - 1 < 7:
                multiply(u - 1)
        quant(8)
        multiply(7)
        multiply(8)
